import numpy as np
import ml_dtypes


def mxq(x, axis, fmt="e4m3"):
    dtype, down = {"e4m3": (ml_dtypes.float8_e4m3fn, 7), "e5m2": (ml_dtypes.float8_e5m2, 14)}[fmt]
    v = np.moveaxis(np.asarray(x, np.float32).astype(ml_dtypes.bfloat16).astype(np.float64), axis, -1)
    blocks = v.reshape(v.shape[:-1] + (-1, 32))
    amax = np.abs(blocks).max(-1, keepdims=True)
    byte = np.maximum(np.where(amax > 0, np.frexp(amax)[1] - 1 + 127, 0) - down, 1)
    scale = np.exp2(byte - 127.0)
    codes = (blocks / scale).astype(np.float32).astype(dtype).astype(np.float64)
    return np.moveaxis((codes * scale).reshape(v.shape), -1, axis)


WIDE = False


def mx_kscale(k):
    if not WIDE:
        return np.ones(k)
    levels = np.array([10, -10, 5, -5, 0])
    a = np.random.permutation(np.resize(levels, k // 512 * 4)).reshape(k // 512, 4)
    idx = np.arange(k)
    return np.exp2(a[idx // 512, idx % 128 // 32])


BF16 = ml_dtypes.bfloat16


def bf(x):
    return np.asarray(x, np.float32).astype(BF16)


def f64(x):
    return np.asarray(x).astype(np.float64)


B, H, W, C, F, KH, KW = 128, 4, 6, 512, 256, 3, 3
OH, OW = H - KH + 1, W - KW + 1
K = KH * KW * C
BN_EPS = 1e-3


def extract_patches(x, kh, kw):
    b, h, w, c = x.shape
    oh, ow = h - kh + 1, w - kw + 1
    slices = [x[:, i:i + oh, j:j + ow, :] for i in range(kh) for j in range(kw)]
    return np.stack(slices, axis=3).reshape(b, oh, ow, kh * kw * c)


def setup_inputs():
    s = mx_kscale(C)
    return {"x": bf(np.random.standard_normal((B, H, W, C)) * 0.14),
            "gamma": bf((1.0 + 0.1 * np.random.standard_normal(C)) * s),
            "beta": bf(0.3 * np.random.standard_normal(C) * s),
            "moving_mean": bf(0.05 * np.random.standard_normal(C)),
            "moving_var": bf(0.01 + 0.02 * np.random.random(C)),
            "weight": bf(np.random.standard_normal((OH * OW, K, F)) / np.sqrt(K) / np.tile(s, KH * KW)[None, :, None])}


def reference(x, gamma, beta, moving_mean, moving_var, weight):
    inv = f64(gamma) / np.sqrt(f64(moving_var) + BN_EPS)
    xn = (f64(x) - f64(moving_mean)) * inv + f64(beta)
    xq = mxq(xn, 3, "e4m3")
    patches = extract_patches(xq, KH, KW)
    p = patches.reshape(B, OH * OW, K).transpose(1, 0, 2)
    y = p @ mxq(f64(weight), 1, "e4m3")
    y = y.transpose(1, 0, 2).reshape(B, OH, OW, F)
    return np.maximum(y, 0.0)

@@ -1,0 +1,144 @@
+from contextlib import ExitStack
+
+import concourse.mybir as mybir
+from concourse.masks import make_identity
+
+F32 = mybir.dt.float32
+BF16 = mybir.dt.bfloat16
+U32 = mybir.dt.uint32
+U8 = mybir.dt.uint8
+FP8X4 = mybir.dt.float8_e4m3fn_x4
+ACT = mybir.ActivationFunctionType
+ALU = mybir.AluOpType
+
+P = 128
+B, H, W, C, F, KH, KW = 128, 4, 6, 512, 256, 3, 3
+OH, OW = H - KH + 1, W - KW + 1
+NPOS = H * W
+TAPS = KH * KW
+NOUT = OH * OW
+UNITS = NOUT * TAPS
+BN_EPS = 1e-3
+FLOPS = 2 * B * NOUT * TAPS * C * F
+
+XG = 4
+CH = 4
+
+
+def regroup_views(dst, src):
+    return (
+        dst.rearrange("p (c i) t -> p c t i", i=4),
+        src.rearrange("p (t c i) -> p c t i", t=4, i=4),
+    )
+
+
+def tile_blockrf_kernel(tc, x, gamma, beta, moving_mean, moving_var, weight, out):
+    nc = tc.nc
+    with ExitStack() as ctx:
+        const = ctx.enter_context(tc.tile_pool(name="const", bufs=1))
+        xwork = ctx.enter_context(tc.tile_pool(name="xwork", bufs=3))
+        rawp = ctx.enter_context(tc.tile_pool(name="rawp", bufs=8))
+        grp = ctx.enter_context(tc.tile_pool(name="grp", bufs=6))
+        codep = ctx.enter_context(tc.tile_pool(name="codep", bufs=8))
+        outp = ctx.enter_context(tc.tile_pool(name="outp", bufs=4))
+        xps = ctx.enter_context(tc.psum_pool(name="xps", bufs=4))
+        accp = ctx.enter_context(tc.psum_pool(name="accp", bufs=3))
+
+        g_t = const.tile([P, 4], BF16, name="g_t")
+        b_t = const.tile([P, 4], BF16, name="b_t")
+        m_t = const.tile([P, 4], BF16, name="m_t")
+        v_t = const.tile([P, 4], BF16, name="v_t")
+        for dst, src in ((v_t, moving_var), (g_t, gamma), (m_t, moving_mean), (b_t, beta)):
+            nc.sync.dma_start(out=dst[:], in_=src.rearrange("(p t) -> p t", t=4))
+
+        x_sb = const.tile([P, NPOS * C], BF16, name="x_sb")
+        x_flat = x.rearrange("b h w c -> b (h w c)")
+        for g in range(NPOS // XG):
+            cols = slice(g * XG * C, (g + 1) * XG * C)
+            nc.sync.dma_start(out=x_sb[:, cols], in_=x_flat[:, cols])
+
+        warm = const.tile([P, 1], F32, name="warm")
+        warm2 = const.tile([P, 1], F32, name="warm2")
+        nc.vector.memset(warm[:], 1.0)
+        nc.scalar.activation(out=warm2[:], in_=warm[:], func=ACT.Sqrt)
+
+        ident = const.tile([P, P], F32, name="ident")
+        make_identity(nc, ident[:])
+
+        veps = const.tile([P, 4], F32, name="veps")
+        sd = const.tile([P, 4], F32, name="sd")
+        rs = const.tile([P, 4], F32, name="rs")
+        inv = const.tile([P, 4], F32, name="inv")
+        mi = const.tile([P, 4], F32, name="mi")
+        shift = const.tile([P, 4], F32, name="shift")
+        nc.vector.tensor_scalar(out=veps[:], in0=v_t[:], scalar1=BN_EPS, scalar2=None, op0=ALU.add)
+        nc.scalar.activation(out=sd[:], in_=veps[:], func=ACT.Sqrt)
+        nc.vector.reciprocal(out=rs[:], in_=sd[:])
+        nc.vector.tensor_tensor(out=inv[:], in0=g_t[:], in1=rs[:], op=ALU.mult)
+        nc.vector.tensor_tensor(out=mi[:], in0=m_t[:], in1=inv[:], op=ALU.mult)
+        nc.vector.tensor_tensor(out=shift[:], in0=b_t[:], in1=mi[:], op=ALU.subtract)
+
+        x_codes = const.tile([P, NPOS * B], U32, name="x_codes", align_bytes=64)
+        x_scales = const.tile([P, NPOS * B], U8, name="x_scales", align_bytes=64)
+        x_words = x_sb[:].bitcast(F32).rearrange("b (q w u) -> b q u w", w=P, u=2)
+        for g in range(NPOS // XG):
+            xn_t = xwork.tile([P, 4, XG * B], BF16, name="xn_t")
+            for u in range(2):
+                xt = xps.tile([P, XG * B], F32, name="xt")
+                for j in range(XG):
+                    nc.tensor.transpose(xt[:, j * B:(j + 1) * B], x_words[:, g * XG + j, u, :], ident[:])
+                halves = xt[:].bitcast(BF16).rearrange("p (n e) -> p n e", e=2)
+                for e in range(2):
+                    t = 2 * u + e
+                    nc.scalar.activation(out=xn_t[:, t, :], in_=halves[:, :, e], func=ACT.Identity,
+                                         bias=shift[:, t:t + 1], scale=inv[:, t:t + 1])
+            gx = xwork.tile([P, XG * B, 4], BF16, name="gx", align_bytes=64)
+            nc.vector.tensor_copy(out=gx[:].rearrange("p (c i) t -> p c t i", i=4),
+                                  in_=xn_t[:].rearrange("p t (c i) -> p c t i", i=4))
+            cols = slice(g * XG * B, (g + 1) * XG * B)
+            nc.vector.quantize_mx(out=x_codes[:, cols].bitcast(FP8X4), scales=x_scales[:, cols],
+                                  in_=gx[:].rearrange("p c t -> p (c t)"))
+
+        w_view = weight.rearrange("o k f -> (o k) f").rearrange("(n p j) f -> p n (j f)", p=P, j=4)
+        out_view = out.rearrange("b h w f -> b (h w) f")
+        state = {"acc": None}
+
+        def quantise_and_multiply(first_unit, gw):
+            wc = codep.tile([P, 2 * F], U32, name="wc", align_bytes=64)
+            ws = codep.tile([P, 2 * F], U8, name="ws", align_bytes=64)
+            nc.vector.quantize_mx(out=wc[:].bitcast(FP8X4), scales=ws[:],
+                                  in_=gw[:].rearrange("p u c t -> p (u c t)"))
+            for k in range(2):
+                o, s = divmod(first_unit + k, TAPS)
+                pos = (o // OW + s // KW) * W + (o % OW + s % KW)
+                if s == 0:
+                    acc = accp.tile([P, F], F32, name="acc")
+                    state["acc"] = acc
+                acc = state["acc"]
+                nc.tensor.matmul_mx(out=acc[:],
+                                    lhsT=x_codes[:, pos * B:(pos + 1) * B].bitcast(FP8X4),
+                                    lhsT_scale=x_scales[:, pos * B:(pos + 1) * B],
+                                    rhs=wc[:, k * F:(k + 1) * F].bitcast(FP8X4),
+                                    rhs_scale=ws[:, k * F:(k + 1) * F],
+                                    start=(s == 0), stop=(s == TAPS - 1))
+                if s == TAPS - 1:
+                    o_sb = outp.tile([P, F], F32, name="o_sb")
+                    nc.scalar.activation(out=o_sb[:], in_=acc[:], func=ACT.Relu)
+                    nc.scalar.dma_start(out=out_view[:, o, :], in_=o_sb[:])
+
+        pending = None
+        for c in range(UNITS // CH):
+            raw = rawp.tile([P, CH, 4 * F], BF16, name="raw")
+            nc.sync.dma_start(out=raw[:], in_=w_view[:, c * CH:(c + 1) * CH, :])
+            gv = grp.tile([P, 2, F, 4], BF16, name="gv", align_bytes=64)
+            nc.vector.tensor_copy(out=gv[:].rearrange("p u (c i) t -> p u c t i", i=4),
+                                  in_=raw[:, 0:2, :].rearrange("p u (t c i) -> p u c t i", t=4, i=4))
+            gs = grp.tile([P, 2, F, 4], BF16, name="gs", align_bytes=64)
+            for k in range(2):
+                dst, src = regroup_views(gs[:, k], raw[:, 2 + k, :])
+                nc.scalar.copy(out=dst, in_=src)
+            if pending is not None:
+                quantise_and_multiply(*pending)
+            quantise_and_multiply(c * CH, gv)
+            pending = (c * CH + 2, gs)
+        quantise_and_multiply(*pending)

@@ -18,52 +18,140 @@ NPOS = H * W
 TAPS = KH * KW
 NOUT = OH * OW
 UNITS = NOUT * TAPS
+NPAIR = UNITS // 2
 BN_EPS = 1e-3
 FLOPS = 2 * B * NOUT * TAPS * C * F
 
 XG = 4
-CH = 4
-
-
-def regroup_views(dst, src):
-    return (
-        dst.rearrange("p (c i) t -> p c t i", i=4),
-        src.rearrange("p (t c i) -> p c t i", t=4, i=4),
-    )
+NG = NPOS // XG
+PIN = False
+RAW4_BUFS = 9
+V_BANKS = ((0, 1), (1, 1))
+PATTERNS = ["SSVV","SSVV","SSVV","SSVV","SSSV","SSVV","SSVV","SSVV","SSVV","SSVV","SSSV","SSVV","SSVV","SSVV","SSVV","SSVV","VVSV"]
+RELU_LAG = 1
 
 
 def tile_blockrf_kernel(tc, x, gamma, beta, moving_mean, moving_var, weight, out):
     nc = tc.nc
     with ExitStack() as ctx:
+        if PIN:
+            ctx.enter_context(tc.manual_schedule())
         const = ctx.enter_context(tc.tile_pool(name="const", bufs=1))
         xwork = ctx.enter_context(tc.tile_pool(name="xwork", bufs=3))
-        rawp = ctx.enter_context(tc.tile_pool(name="rawp", bufs=8))
-        grp = ctx.enter_context(tc.tile_pool(name="grp", bufs=6))
+        raw4p = ctx.enter_context(tc.tile_pool(name="raw4p", bufs=RAW4_BUFS))
+        raw2p = ctx.enter_context(tc.tile_pool(name="raw2p", bufs=2))
+        grp = ctx.enter_context(tc.tile_pool(name="grp", bufs=4))
         codep = ctx.enter_context(tc.tile_pool(name="codep", bufs=8))
         outp = ctx.enter_context(tc.tile_pool(name="outp", bufs=4))
         xps = ctx.enter_context(tc.psum_pool(name="xps", bufs=4))
-        accp = ctx.enter_context(tc.psum_pool(name="accp", bufs=3))
+        accp = ctx.enter_context(tc.psum_pool(name="accp", bufs=4))
+
+        w_view = weight.rearrange("o k f -> (o k) f").rearrange("(n p j) f -> p n (j f)", p=P, j=4)
+        out_view = out.rearrange("b h w f -> b (h w) f")
+        x_flat = x.rearrange("b h w c -> b (h w c)")
+
+        tiles = [(0, 2, 2), (2, 2, 1)] + [(4 + 4 * k, 4, 1) for k in range(16)] + [(68, 2, 1), (70, 2, 2)]
+        raw_of_unit = {}
+
+        def load_tile(k):
+            first, n, dmas = tiles[k]
+            if n == 4:
+                raw = raw4p.tile([P, 4, 4 * F], BF16, name="raw4")
+            else:
+                raw = raw2p.tile([P, 2, 4 * F], BF16, name="raw2")
+            step = n // dmas
+            for d in range(dmas):
+                nc.sync.dma_start(out=raw[:, d * step:(d + 1) * step, :],
+                                  in_=w_view[:, first + d * step:first + (d + 1) * step, :])
+            for u in range(n):
+                raw_of_unit[first + u] = raw[:, u, :]
+            for u in range(0, n, 2):
+                raw_of_unit[(first + u, 2)] = raw[:, u:u + 2, :]
 
         g_t = const.tile([P, 4], BF16, name="g_t")
         b_t = const.tile([P, 4], BF16, name="b_t")
         m_t = const.tile([P, 4], BF16, name="m_t")
         v_t = const.tile([P, 4], BF16, name="v_t")
         for dst, src in ((v_t, moving_var), (g_t, gamma), (m_t, moving_mean), (b_t, beta)):
-            nc.sync.dma_start(out=dst[:], in_=src.rearrange("(p t) -> p t", t=4))
-
+            nc.scalar.dma_start(out=dst[:], in_=src.rearrange("(p t) -> p t", t=4))
+        load_tile(0)
         x_sb = const.tile([P, NPOS * C], BF16, name="x_sb")
-        x_flat = x.rearrange("b h w c -> b (h w c)")
-        for g in range(NPOS // XG):
+        for g in range(NG):
             cols = slice(g * XG * C, (g + 1) * XG * C)
             nc.sync.dma_start(out=x_sb[:, cols], in_=x_flat[:, cols])
+        next_tile = 1
+        while next_tile < 2 + RAW4_BUFS:
+            load_tile(next_tile)
+            next_tile += 1
 
         warm = const.tile([P, 1], F32, name="warm")
         warm2 = const.tile([P, 1], F32, name="warm2")
         nc.vector.memset(warm[:], 1.0)
         nc.scalar.activation(out=warm2[:], in_=warm[:], func=ACT.Sqrt)
-
         ident = const.tile([P, P], F32, name="ident")
         make_identity(nc, ident[:])
+
+        def regroup_v_unit(dst, unit):
+            nc.vector.tensor_copy(out=dst.rearrange("p (c i) t -> p c t i", i=4),
+                                  in_=raw_of_unit[unit].rearrange("p (t c i) -> p c t i", t=4, i=4))
+
+        def regroup_s_unit(dst, unit):
+            nc.scalar.copy(out=dst.rearrange("p (c i) t -> p c t i", i=4),
+                           in_=raw_of_unit[unit].rearrange("p (t c i) -> p c t i", t=4, i=4))
+
+        def regroup_v_pair(pair):
+            gv = grp.tile([P, 2, F, 4], BF16, name="gv", align_bytes=64)
+            nc.vector.tensor_copy(out=gv[:].rearrange("p u (c i) t -> p u c t i", i=4),
+                                  in_=raw_of_unit[(2 * pair, 2)].rearrange("p u (t c i) -> p u c t i", t=4, i=4))
+            return gv
+
+        def regroup_s_pair(pair):
+            gs = grp.tile([P, 2, F, 4], BF16, name="gs", align_bytes=64)
+            for k in range(2):
+                regroup_s_unit(gs[:, k], 2 * pair + k)
+            return gs
+
+        def quantise(gw):
+            wc = codep.tile([P, 2 * F], U32, name="wc", align_bytes=64)
+            ws = codep.tile([P, 2 * F], U8, name="ws", align_bytes=64)
+            nc.vector.quantize_mx(out=wc[:].bitcast(FP8X4), scales=ws[:],
+                                  in_=gw[:].rearrange("p u c t -> p (u c t)"))
+            return wc, ws
+
+        x_codes = const.tile([P, NPOS * B], U32, name="x_codes", align_bytes=64)
+        x_scales = const.tile([P, NPOS * B], U8, name="x_scales", align_bytes=64)
+        accs = {}
+        relus = []
+
+        def multiply(pair, wc, ws):
+            for k in range(2):
+                o, s = divmod(2 * pair + k, TAPS)
+                pos = (o // OW + s // KW) * W + (o % OW + s % KW)
+                if s == 0:
+                    acc = accp.tile([P, F], F32, name="acc")
+                    accs[o] = acc
+                nc.tensor.matmul_mx(out=accs[o][:],
+                                    lhsT=x_codes[:, pos * B:(pos + 1) * B].bitcast(FP8X4),
+                                    lhsT_scale=x_scales[:, pos * B:(pos + 1) * B],
+                                    rhs=wc[:, k * F:(k + 1) * F].bitcast(FP8X4),
+                                    rhs_scale=ws[:, k * F:(k + 1) * F],
+                                    start=(s == 0), stop=(s == TAPS - 1))
+                if s == TAPS - 1:
+                    relus.append([o, RELU_LAG])
+
+        flushed = {"n": 0}
+
+        def flush_relus(force=False):
+            for idx in range(flushed["n"], len(relus)):
+                item = relus[idx]
+                if force or item[1] <= 0:
+                    o = item[0]
+                    o_sb = outp.tile([P, F], F32, name="o_sb")
+                    nc.scalar.activation(out=o_sb[:], in_=accs[o][:], func=ACT.Relu)
+                    nc.scalar.dma_start(out=out_view[:, o, :], in_=o_sb[:])
+                    flushed["n"] = idx + 1
+                else:
+                    item[1] -= 1
 
         veps = const.tile([P, 4], F32, name="veps")
         sd = const.tile([P, 4], F32, name="sd")
@@ -73,72 +161,109 @@ def tile_blockrf_kernel(tc, x, gamma, beta, moving_mean, moving_var, weight, out
         shift = const.tile([P, 4], F32, name="shift")
         nc.vector.tensor_scalar(out=veps[:], in0=v_t[:], scalar1=BN_EPS, scalar2=None, op0=ALU.add)
         nc.scalar.activation(out=sd[:], in_=veps[:], func=ACT.Sqrt)
+        g0 = grp.tile([P, 2, F, 4], BF16, name="gv", align_bytes=64)
+        regroup_v_unit(g0[:, 0], 0)
+        regroup_s_unit(g0[:, 1], 1)
         nc.vector.reciprocal(out=rs[:], in_=sd[:])
         nc.vector.tensor_tensor(out=inv[:], in0=g_t[:], in1=rs[:], op=ALU.mult)
         nc.vector.tensor_tensor(out=mi[:], in0=m_t[:], in1=inv[:], op=ALU.mult)
         nc.vector.tensor_tensor(out=shift[:], in0=b_t[:], in1=mi[:], op=ALU.subtract)
 
-        x_codes = const.tile([P, NPOS * B], U32, name="x_codes", align_bytes=64)
-        x_scales = const.tile([P, NPOS * B], U8, name="x_scales", align_bytes=64)
         x_words = x_sb[:].bitcast(F32).rearrange("b (q w u) -> b q u w", w=P, u=2)
-        for g in range(NPOS // XG):
-            xn_t = xwork.tile([P, 4, XG * B], BF16, name="xn_t")
+        banks = {}
+
+        def transposes(g):
             for u in range(2):
                 xt = xps.tile([P, XG * B], F32, name="xt")
                 for j in range(XG):
                     nc.tensor.transpose(xt[:, j * B:(j + 1) * B], x_words[:, g * XG + j, u, :], ident[:])
-                halves = xt[:].bitcast(BF16).rearrange("p (n e) -> p n e", e=2)
+                banks[(g, u)] = xt
+
+        xn = {}
+
+        def batch_norm(g):
+            xn_t = xwork.tile([P, 4, XG * B], BF16, name="xn_t")
+            xn[g] = xn_t
+            for u in range(2):
+                halves = banks[(g, u)][:].bitcast(BF16).rearrange("p (n e) -> p n e", e=2)
                 for e in range(2):
                     t = 2 * u + e
-                    nc.scalar.activation(out=xn_t[:, t, :], in_=halves[:, :, e], func=ACT.Identity,
-                                         bias=shift[:, t:t + 1], scale=inv[:, t:t + 1])
+                    if (g, u) in V_BANKS:
+                        nc.vector.tensor_scalar(out=xn_t[:, t, :], in0=halves[:, :, e],
+                                                scalar1=inv[:, t:t + 1], scalar2=shift[:, t:t + 1],
+                                                op0=ALU.mult, op1=ALU.add)
+                    else:
+                        nc.scalar.activation(out=xn_t[:, t, :], in_=halves[:, :, e], func=ACT.Identity,
+                                             bias=shift[:, t:t + 1], scale=inv[:, t:t + 1])
+
+        gxs = {}
+
+        def x_regroup(g):
             gx = xwork.tile([P, XG * B, 4], BF16, name="gx", align_bytes=64)
+            gxs[g] = gx
             nc.vector.tensor_copy(out=gx[:].rearrange("p (c i) t -> p c t i", i=4),
-                                  in_=xn_t[:].rearrange("p t (c i) -> p c t i", i=4))
+                                  in_=xn[g][:].rearrange("p t (c i) -> p c t i", i=4))
+
+        def x_quantise(g):
             cols = slice(g * XG * B, (g + 1) * XG * B)
             nc.vector.quantize_mx(out=x_codes[:, cols].bitcast(FP8X4), scales=x_scales[:, cols],
-                                  in_=gx[:].rearrange("p c t -> p (c t)"))
+                                  in_=gxs[g][:].rearrange("p c t -> p (c t)"))
 
-        w_view = weight.rearrange("o k f -> (o k) f").rearrange("(n p j) f -> p n (j f)", p=P, j=4)
-        out_view = out.rearrange("b h w f -> b (h w) f")
-        state = {"acc": None}
+        transposes(0)
+        transposes(1)
+        batch_norm(0)
+        transposes(2)
+        q0 = quantise(g0)
+        x_regroup(0)
+        batch_norm(1)
+        transposes(3)
+        x_regroup(1)
+        x_quantise(0)
+        g1 = regroup_v_pair(1)
+        batch_norm(2)
+        transposes(4)
+        x_regroup(2)
+        x_quantise(1)
+        q1 = quantise(g1)
+        batch_norm(3)
+        transposes(5)
+        x_regroup(3)
+        x_quantise(2)
+        batch_norm(4)
+        x_regroup(4)
+        x_quantise(3)
+        batch_norm(5)
+        x_regroup(5)
+        x_quantise(4)
 
-        def quantise_and_multiply(first_unit, gw):
-            wc = codep.tile([P, 2 * F], U32, name="wc", align_bytes=64)
-            ws = codep.tile([P, 2 * F], U8, name="ws", align_bytes=64)
-            nc.vector.quantize_mx(out=wc[:].bitcast(FP8X4), scales=ws[:],
-                                  in_=gw[:].rearrange("p u c t -> p (u c t)"))
+        def regroup_pair(pair, engines):
+            if engines == "VV":
+                return regroup_v_pair(pair)
+            if engines == "SS":
+                return regroup_s_pair(pair)
+            gm = grp.tile([P, 2, F, 4], BF16, name="gm", align_bytes=64)
             for k in range(2):
-                o, s = divmod(first_unit + k, TAPS)
-                pos = (o // OW + s // KW) * W + (o % OW + s % KW)
-                if s == 0:
-                    acc = accp.tile([P, F], F32, name="acc")
-                    state["acc"] = acc
-                acc = state["acc"]
-                nc.tensor.matmul_mx(out=acc[:],
-                                    lhsT=x_codes[:, pos * B:(pos + 1) * B].bitcast(FP8X4),
-                                    lhsT_scale=x_scales[:, pos * B:(pos + 1) * B],
-                                    rhs=wc[:, k * F:(k + 1) * F].bitcast(FP8X4),
-                                    rhs_scale=ws[:, k * F:(k + 1) * F],
-                                    start=(s == 0), stop=(s == TAPS - 1))
-                if s == TAPS - 1:
-                    o_sb = outp.tile([P, F], F32, name="o_sb")
-                    nc.scalar.activation(out=o_sb[:], in_=acc[:], func=ACT.Relu)
-                    nc.scalar.dma_start(out=out_view[:, o, :], in_=o_sb[:])
-
-        pending = None
-        for c in range(UNITS // CH):
-            raw = rawp.tile([P, CH, 4 * F], BF16, name="raw")
-            nc.sync.dma_start(out=raw[:], in_=w_view[:, c * CH:(c + 1) * CH, :])
-            gv = grp.tile([P, 2, F, 4], BF16, name="gv", align_bytes=64)
-            nc.vector.tensor_copy(out=gv[:].rearrange("p u (c i) t -> p u c t i", i=4),
-                                  in_=raw[:, 0:2, :].rearrange("p u (t c i) -> p u c t i", t=4, i=4))
-            gs = grp.tile([P, 2, F, 4], BF16, name="gs", align_bytes=64)
+                if engines[k] == "S":
+                    regroup_s_unit(gm[:, k], 2 * pair + k)
             for k in range(2):
-                dst, src = regroup_views(gs[:, k], raw[:, 2 + k, :])
-                nc.scalar.copy(out=dst, in_=src)
-            if pending is not None:
-                quantise_and_multiply(*pending)
-            quantise_and_multiply(c * CH, gv)
-            pending = (c * CH + 2, gs)
-        quantise_and_multiply(*pending)
+                if engines[k] == "V":
+                    regroup_v_unit(gm[:, k], 2 * pair + k)
+            return gm
+
+        first = True
+        for i in range(1, 18):
+            pat = PATTERNS[i - 1]
+            ga = regroup_pair(2 * i, pat[0:2])
+            gb = regroup_pair(2 * i + 1, pat[2:4])
+            if next_tile < len(tiles):
+                load_tile(next_tile)
+                next_tile += 1
+            if first:
+                x_quantise(5)
+                multiply(0, *q0)
+                multiply(1, *q1)
+                first = False
+            flush_relus(force=(i == 17))
+            multiply(2 * i, *quantise(ga))
+            multiply(2 * i + 1, *quantise(gb))
+        flush_relus(force=True)

@@ -27,7 +27,7 @@ NG = NPOS // XG
 PIN = False
 RAW4_BUFS = 9
 V_BANKS = ((0, 1), (1, 1))
-PATTERNS = ["SSVV","SSVV","SSVV","SSVV","SSSV","SSVV","SSVV","SSVV","SSVV","SSVV","SSSV","SSVV","SSVV","SSVV","SSVV","SSVV","VVSV"]
+PATTERNS = ["SSVV","SSVV","SSVV","SSVV","SSVV","SVVV","SSVV","SSVV","SSVV","SSVV","SSVV","SSVV","SSVV","SSVV","SSVV","SSVV","VVSV"]
 RELU_LAG = 1
 
 

@@ -27,7 +27,7 @@ NG = NPOS // XG
 PIN = False
 RAW4_BUFS = 9
 V_BANKS = ((0, 1), (1, 1))
-PATTERNS = ["SSVV","SSVV","SSVV","SSVV","SSVV","SVVV","SSVV","SSVV","SSVV","SSVV","SSVV","SSVV","SSVV","SSVV","SSVV","SSVV","VVSV"]
+PATTERNS = ["SSVV","SSVV","SSVV","SSVV","SSVV","SSVV","SSVV","SSSV","SSVV","SSVV","SSVV","SSVV","SSVV","SSVV","SSVV","SSVV","VVSV"]
 RELU_LAG = 1
 
 

@@ -24,10 +24,10 @@ FLOPS = 2 * B * NOUT * TAPS * C * F
 
 XG = 4
 NG = NPOS // XG
-PIN = False
+PIN = True
 RAW4_BUFS = 9
 V_BANKS = ((0, 1), (1, 1))
-PATTERNS = ["SSVV","SSVV","SSVV","SSVV","SSVV","SSVV","SSVV","SSSV","SSVV","SSVV","SSVV","SSVV","SSVV","SSVV","SSVV","SSVV","VVSV"]
+PATTERNS = ["SSVV","SSVV","SSVV","SSVV","SSVV","SSVV","SSVV","SSVV","SSVV","SSVV","SSVV","SSVV","SSVV","SSVV","SSVV","SSVV","SSSV"]
 RELU_LAG = 1
 
 
@@ -148,7 +148,7 @@ def tile_blockrf_kernel(tc, x, gamma, beta, moving_mean, moving_var, weight, out
                     o = item[0]
                     o_sb = outp.tile([P, F], F32, name="o_sb")
                     nc.scalar.activation(out=o_sb[:], in_=accs[o][:], func=ACT.Relu)
-                    nc.scalar.dma_start(out=out_view[:, o, :], in_=o_sb[:])
+                    nc.sync.dma_start(out=out_view[:, o, :], in_=o_sb[:])
                     flushed["n"] = idx + 1
                 else:
                     item[1] -= 1
@@ -211,9 +211,9 @@ def tile_blockrf_kernel(tc, x, gamma, beta, moving_mean, moving_var, weight, out
 
         transposes(0)
         transposes(1)
+        q0 = quantise(g0)
         batch_norm(0)
         transposes(2)
-        q0 = quantise(g0)
         x_regroup(0)
         batch_norm(1)
         transposes(3)

@@ -12,77 +12,82 @@ ACT = mybir.ActivationFunctionType
 ALU = mybir.AluOpType
 
 P = 128
+PACK = 4
 B, H, W, C, F, KH, KW = 128, 4, 6, 512, 256, 3, 3
 OH, OW = H - KH + 1, W - KW + 1
 NPOS = H * W
 TAPS = KH * KW
 NOUT = OH * OW
 UNITS = NOUT * TAPS
-NPAIR = UNITS // 2
 BN_EPS = 1e-3
 FLOPS = 2 * B * NOUT * TAPS * C * F
 
 XG = 4
 NG = NPOS // XG
-PIN = True
-RAW4_BUFS = 9
+HEAD_UNITS = 4
+TAIL_UNITS = 4
+BLOCK = 4
+NBLOCK = (UNITS - HEAD_UNITS - TAIL_UNITS) // BLOCK
+RAW_BUFS = 7
 V_BANKS = ((0, 1), (1, 1))
-PATTERNS = ["SSVV","SSVV","SSVV","SSVV","SSVV","SSVV","SSVV","SSVV","SSVV","SSVV","SSVV","SSVV","SSVV","SSVV","SSVV","SSVV","SSSV"]
-RELU_LAG = 1
+RELU_LAG = 2
+
+
+def by_column(grouped):
+    return grouped.rearrange("p (c i) t -> p c t i", i=4)
+
+
+def by_row(raw):
+    return raw.rearrange("p (t c i) -> p c t i", t=PACK, i=4)
 
 
 def tile_blockrf_kernel(tc, x, gamma, beta, moving_mean, moving_var, weight, out):
     nc = tc.nc
     with ExitStack() as ctx:
-        if PIN:
-            ctx.enter_context(tc.manual_schedule())
+        ctx.enter_context(tc.manual_schedule())
         const = ctx.enter_context(tc.tile_pool(name="const", bufs=1))
         xwork = ctx.enter_context(tc.tile_pool(name="xwork", bufs=3))
-        raw4p = ctx.enter_context(tc.tile_pool(name="raw4p", bufs=RAW4_BUFS))
+        rawp = ctx.enter_context(tc.tile_pool(name="rawp", bufs=RAW_BUFS))
         raw2p = ctx.enter_context(tc.tile_pool(name="raw2p", bufs=2))
         grp = ctx.enter_context(tc.tile_pool(name="grp", bufs=4))
-        codep = ctx.enter_context(tc.tile_pool(name="codep", bufs=8))
+        grp2 = ctx.enter_context(tc.tile_pool(name="grp2", bufs=2))
+        codep = ctx.enter_context(tc.tile_pool(name="codep", bufs=4))
+        code2p = ctx.enter_context(tc.tile_pool(name="code2p", bufs=2))
         outp = ctx.enter_context(tc.tile_pool(name="outp", bufs=4))
         xps = ctx.enter_context(tc.psum_pool(name="xps", bufs=4))
         accp = ctx.enter_context(tc.psum_pool(name="accp", bufs=4))
 
-        w_view = weight.rearrange("o k f -> (o k) f").rearrange("(n p j) f -> p n (j f)", p=P, j=4)
+        w_view = weight.rearrange("o k f -> (o k) f").rearrange("(n p j) f -> p n (j f)", p=P, j=PACK)
         out_view = out.rearrange("b h w f -> b (h w) f")
         x_flat = x.rearrange("b h w c -> b (h w c)")
 
-        tiles = [(0, 2, 2), (2, 2, 1)] + [(4 + 4 * k, 4, 1) for k in range(16)] + [(68, 2, 1), (70, 2, 2)]
-        raw_of_unit = {}
-
-        def load_tile(k):
-            first, n, dmas = tiles[k]
-            if n == 4:
-                raw = raw4p.tile([P, 4, 4 * F], BF16, name="raw4")
-            else:
-                raw = raw2p.tile([P, 2, 4 * F], BF16, name="raw2")
-            step = n // dmas
+        def load_pair(first, dmas):
+            raw = raw2p.tile([P, 2, PACK * F], BF16, name="raw2")
+            step = 2 // dmas
             for d in range(dmas):
                 nc.sync.dma_start(out=raw[:, d * step:(d + 1) * step, :],
                                   in_=w_view[:, first + d * step:first + (d + 1) * step, :])
-            for u in range(n):
-                raw_of_unit[first + u] = raw[:, u, :]
-            for u in range(0, n, 2):
-                raw_of_unit[(first + u, 2)] = raw[:, u:u + 2, :]
+            return raw
 
-        g_t = const.tile([P, 4], BF16, name="g_t")
-        b_t = const.tile([P, 4], BF16, name="b_t")
-        m_t = const.tile([P, 4], BF16, name="m_t")
-        v_t = const.tile([P, 4], BF16, name="v_t")
+        def load_block(b):
+            raw = rawp.tile([P, BLOCK, PACK * F], BF16, name="raw")
+            first = HEAD_UNITS + b * BLOCK
+            nc.sync.dma_start(out=raw[:], in_=w_view[:, first:first + BLOCK, :])
+            return raw
+
+        g_t = const.tile([P, PACK], BF16, name="g_t")
+        b_t = const.tile([P, PACK], BF16, name="b_t")
+        m_t = const.tile([P, PACK], BF16, name="m_t")
+        v_t = const.tile([P, PACK], BF16, name="v_t")
         for dst, src in ((v_t, moving_var), (g_t, gamma), (m_t, moving_mean), (b_t, beta)):
-            nc.scalar.dma_start(out=dst[:], in_=src.rearrange("(p t) -> p t", t=4))
-        load_tile(0)
+            nc.scalar.dma_start(out=dst[:], in_=src.rearrange("(p t) -> p t", t=PACK))
+        raw_h0 = load_pair(0, 2)
         x_sb = const.tile([P, NPOS * C], BF16, name="x_sb")
         for g in range(NG):
             cols = slice(g * XG * C, (g + 1) * XG * C)
             nc.sync.dma_start(out=x_sb[:, cols], in_=x_flat[:, cols])
-        next_tile = 1
-        while next_tile < 2 + RAW4_BUFS:
-            load_tile(next_tile)
-            next_tile += 1
+        raw_h1 = load_pair(2, 1)
+        raws = [load_block(b) for b in range(RAW_BUFS)]
 
         warm = const.tile([P, 1], F32, name="warm")
         warm2 = const.tile([P, 1], F32, name="warm2")
@@ -91,79 +96,55 @@ def tile_blockrf_kernel(tc, x, gamma, beta, moving_mean, moving_var, weight, out
         ident = const.tile([P, P], F32, name="ident")
         make_identity(nc, ident[:])
 
-        def regroup_v_unit(dst, unit):
-            nc.vector.tensor_copy(out=dst.rearrange("p (c i) t -> p c t i", i=4),
-                                  in_=raw_of_unit[unit].rearrange("p (t c i) -> p c t i", t=4, i=4))
-
-        def regroup_s_unit(dst, unit):
-            nc.scalar.copy(out=dst.rearrange("p (c i) t -> p c t i", i=4),
-                           in_=raw_of_unit[unit].rearrange("p (t c i) -> p c t i", t=4, i=4))
-
-        def regroup_v_pair(pair):
-            gv = grp.tile([P, 2, F, 4], BF16, name="gv", align_bytes=64)
-            nc.vector.tensor_copy(out=gv[:].rearrange("p u (c i) t -> p u c t i", i=4),
-                                  in_=raw_of_unit[(2 * pair, 2)].rearrange("p u (t c i) -> p u c t i", t=4, i=4))
-            return gv
-
-        def regroup_s_pair(pair):
-            gs = grp.tile([P, 2, F, 4], BF16, name="gs", align_bytes=64)
-            for k in range(2):
-                regroup_s_unit(gs[:, k], 2 * pair + k)
-            return gs
-
-        def quantise(gw):
-            wc = codep.tile([P, 2 * F], U32, name="wc", align_bytes=64)
-            ws = codep.tile([P, 2 * F], U8, name="ws", align_bytes=64)
-            nc.vector.quantize_mx(out=wc[:].bitcast(FP8X4), scales=ws[:],
-                                  in_=gw[:].rearrange("p u c t -> p (u c t)"))
-            return wc, ws
-
         x_codes = const.tile([P, NPOS * B], U32, name="x_codes", align_bytes=64)
         x_scales = const.tile([P, NPOS * B], U8, name="x_scales", align_bytes=64)
         accs = {}
-        relus = []
+        finished = []
+        stored = {"n": 0}
 
-        def multiply(pair, wc, ws):
-            for k in range(2):
-                o, s = divmod(2 * pair + k, TAPS)
-                pos = (o // OW + s // KW) * W + (o % OW + s % KW)
-                if s == 0:
+        def quantise(grouped, units, pool):
+            codes = pool.tile([P, units * F], U32, name="codes%d" % units, align_bytes=64)
+            scales = pool.tile([P, units * F], U8, name="scales%d" % units, align_bytes=64)
+            nc.vector.quantize_mx(out=codes[:].bitcast(FP8X4), scales=scales[:],
+                                  in_=grouped[:].rearrange("p u c t -> p (u c t)"))
+            return codes, scales
+
+        def multiply(first, units, codes, scales, step):
+            for k in range(units):
+                o, tap = divmod(first + k, TAPS)
+                pos = (o // OW + tap // KW) * W + (o % OW + tap % KW)
+                if tap == 0:
                     acc = accp.tile([P, F], F32, name="acc")
                     accs[o] = acc
                 nc.tensor.matmul_mx(out=accs[o][:],
                                     lhsT=x_codes[:, pos * B:(pos + 1) * B].bitcast(FP8X4),
                                     lhsT_scale=x_scales[:, pos * B:(pos + 1) * B],
-                                    rhs=wc[:, k * F:(k + 1) * F].bitcast(FP8X4),
-                                    rhs_scale=ws[:, k * F:(k + 1) * F],
-                                    start=(s == 0), stop=(s == TAPS - 1))
-                if s == TAPS - 1:
-                    relus.append([o, RELU_LAG])
+                                    rhs=codes[:, k * F:(k + 1) * F].bitcast(FP8X4),
+                                    rhs_scale=scales[:, k * F:(k + 1) * F],
+                                    start=(tap == 0), stop=(tap == TAPS - 1))
+                if tap == TAPS - 1:
+                    finished.append((o, step))
 
-        flushed = {"n": 0}
-
-        def flush_relus(force=False):
-            for idx in range(flushed["n"], len(relus)):
-                item = relus[idx]
-                if force or item[1] <= 0:
-                    o = item[0]
+        def relu_and_store(step):
+            for idx in range(stored["n"], len(finished)):
+                o, when = finished[idx]
+                if step - when >= RELU_LAG:
                     o_sb = outp.tile([P, F], F32, name="o_sb")
                     nc.scalar.activation(out=o_sb[:], in_=accs[o][:], func=ACT.Relu)
                     nc.sync.dma_start(out=out_view[:, o, :], in_=o_sb[:])
-                    flushed["n"] = idx + 1
-                else:
-                    item[1] -= 1
+                    stored["n"] = idx + 1
 
-        veps = const.tile([P, 4], F32, name="veps")
-        sd = const.tile([P, 4], F32, name="sd")
-        rs = const.tile([P, 4], F32, name="rs")
-        inv = const.tile([P, 4], F32, name="inv")
-        mi = const.tile([P, 4], F32, name="mi")
-        shift = const.tile([P, 4], F32, name="shift")
+        veps = const.tile([P, PACK], F32, name="veps")
+        sd = const.tile([P, PACK], F32, name="sd")
+        rs = const.tile([P, PACK], F32, name="rs")
+        inv = const.tile([P, PACK], F32, name="inv")
+        mi = const.tile([P, PACK], F32, name="mi")
+        shift = const.tile([P, PACK], F32, name="shift")
         nc.vector.tensor_scalar(out=veps[:], in0=v_t[:], scalar1=BN_EPS, scalar2=None, op0=ALU.add)
         nc.scalar.activation(out=sd[:], in_=veps[:], func=ACT.Sqrt)
-        g0 = grp.tile([P, 2, F, 4], BF16, name="gv", align_bytes=64)
-        regroup_v_unit(g0[:, 0], 0)
-        regroup_s_unit(g0[:, 1], 1)
+        g_h0 = grp2.tile([P, 2, F, PACK], BF16, name="g2", align_bytes=64)
+        nc.vector.tensor_copy(out=by_column(g_h0[:, 0]), in_=by_row(raw_h0[:, 0, :]))
+        nc.scalar.copy(out=by_column(g_h0[:, 1]), in_=by_row(raw_h0[:, 1, :]))
         nc.vector.reciprocal(out=rs[:], in_=sd[:])
         nc.vector.tensor_tensor(out=inv[:], in0=g_t[:], in1=rs[:], op=ALU.mult)
         nc.vector.tensor_tensor(out=mi[:], in0=m_t[:], in1=inv[:], op=ALU.mult)
@@ -171,6 +152,8 @@ def tile_blockrf_kernel(tc, x, gamma, beta, moving_mean, moving_var, weight, out
 
         x_words = x_sb[:].bitcast(F32).rearrange("b (q w u) -> b q u w", w=P, u=2)
         banks = {}
+        xn = {}
+        gxs = {}
 
         def transposes(g):
             for u in range(2):
@@ -179,10 +162,8 @@ def tile_blockrf_kernel(tc, x, gamma, beta, moving_mean, moving_var, weight, out
                     nc.tensor.transpose(xt[:, j * B:(j + 1) * B], x_words[:, g * XG + j, u, :], ident[:])
                 banks[(g, u)] = xt
 
-        xn = {}
-
         def batch_norm(g):
-            xn_t = xwork.tile([P, 4, XG * B], BF16, name="xn_t")
+            xn_t = xwork.tile([P, PACK, XG * B], BF16, name="xn_t")
             xn[g] = xn_t
             for u in range(2):
                 halves = banks[(g, u)][:].bitcast(BF16).rearrange("p (n e) -> p n e", e=2)
@@ -196,13 +177,10 @@ def tile_blockrf_kernel(tc, x, gamma, beta, moving_mean, moving_var, weight, out
                         nc.scalar.activation(out=xn_t[:, t, :], in_=halves[:, :, e], func=ACT.Identity,
                                              bias=shift[:, t:t + 1], scale=inv[:, t:t + 1])
 
-        gxs = {}
-
         def x_regroup(g):
-            gx = xwork.tile([P, XG * B, 4], BF16, name="gx", align_bytes=64)
+            gx = xwork.tile([P, XG * B, PACK], BF16, name="gx", align_bytes=64)
             gxs[g] = gx
-            nc.vector.tensor_copy(out=gx[:].rearrange("p (c i) t -> p c t i", i=4),
-                                  in_=xn[g][:].rearrange("p t (c i) -> p c t i", i=4))
+            nc.vector.tensor_copy(out=by_column(gx[:]), in_=xn[g][:].rearrange("p t (c i) -> p c t i", i=4))
 
         def x_quantise(g):
             cols = slice(g * XG * B, (g + 1) * XG * B)
@@ -211,7 +189,7 @@ def tile_blockrf_kernel(tc, x, gamma, beta, moving_mean, moving_var, weight, out
 
         transposes(0)
         transposes(1)
-        q0 = quantise(g0)
+        q_h0 = quantise(g_h0, 2, code2p)
         batch_norm(0)
         transposes(2)
         x_regroup(0)
@@ -219,12 +197,14 @@ def tile_blockrf_kernel(tc, x, gamma, beta, moving_mean, moving_var, weight, out
         transposes(3)
         x_regroup(1)
         x_quantise(0)
-        g1 = regroup_v_pair(1)
+        g_h1 = grp2.tile([P, 2, F, PACK], BF16, name="g2", align_bytes=64)
+        nc.vector.tensor_copy(out=g_h1[:].rearrange("p u (c i) t -> p u c t i", i=4),
+                              in_=raw_h1[:].rearrange("p u (t c i) -> p u c t i", t=PACK, i=4))
         batch_norm(2)
         transposes(4)
         x_regroup(2)
         x_quantise(1)
-        q1 = quantise(g1)
+        q_h1 = quantise(g_h1, 2, code2p)
         batch_norm(3)
         transposes(5)
         x_regroup(3)
@@ -236,34 +216,42 @@ def tile_blockrf_kernel(tc, x, gamma, beta, moving_mean, moving_var, weight, out
         x_regroup(5)
         x_quantise(4)
 
-        def regroup_pair(pair, engines):
-            if engines == "VV":
-                return regroup_v_pair(pair)
-            if engines == "SS":
-                return regroup_s_pair(pair)
-            gm = grp.tile([P, 2, F, 4], BF16, name="gm", align_bytes=64)
+        tail_raws = []
+        previous = None
+        for b in range(NBLOCK):
+            raw = raws[b]
+            g4 = grp.tile([P, BLOCK, F, PACK], BF16, name="g4", align_bytes=64)
             for k in range(2):
-                if engines[k] == "S":
-                    regroup_s_unit(gm[:, k], 2 * pair + k)
-            for k in range(2):
-                if engines[k] == "V":
-                    regroup_v_unit(gm[:, k], 2 * pair + k)
-            return gm
-
-        first = True
-        for i in range(1, 18):
-            pat = PATTERNS[i - 1]
-            ga = regroup_pair(2 * i, pat[0:2])
-            gb = regroup_pair(2 * i + 1, pat[2:4])
-            if next_tile < len(tiles):
-                load_tile(next_tile)
-                next_tile += 1
-            if first:
+                nc.scalar.copy(out=by_column(g4[:, k]), in_=by_row(raw[:, k, :]))
+            nc.vector.tensor_copy(out=g4[:, 2:4].rearrange("p u (c i) t -> p u c t i", i=4),
+                                  in_=raw[:, 2:4, :].rearrange("p u (t c i) -> p u c t i", t=PACK, i=4))
+            if b + RAW_BUFS < NBLOCK:
+                raws.append(load_block(b + RAW_BUFS))
+            elif len(tail_raws) == 0:
+                tail_raws.append(load_pair(UNITS - 4, 1))
+            elif len(tail_raws) == 1:
+                tail_raws.append(load_pair(UNITS - 2, 2))
+            if b == 0:
                 x_quantise(5)
-                multiply(0, *q0)
-                multiply(1, *q1)
-                first = False
-            flush_relus(force=(i == 17))
-            multiply(2 * i, *quantise(ga))
-            multiply(2 * i + 1, *quantise(gb))
-        flush_relus(force=True)
+                multiply(0, 2, q_h0[0], q_h0[1], b)
+                multiply(2, 2, q_h1[0], q_h1[1], b)
+            relu_and_store(b)
+            if previous is not None:
+                codes, scales = quantise(previous, BLOCK, codep)
+                multiply(HEAD_UNITS + (b - 1) * BLOCK, BLOCK, codes, scales, b)
+            previous = g4
+
+        g_t0 = grp2.tile([P, 2, F, PACK], BF16, name="g2", align_bytes=64)
+        g_t1 = grp2.tile([P, 2, F, PACK], BF16, name="g2", align_bytes=64)
+        for k in range(2):
+            nc.scalar.copy(out=by_column(g_t0[:, k]), in_=by_row(tail_raws[0][:, k, :]))
+        nc.scalar.copy(out=by_column(g_t1[:, 0]), in_=by_row(tail_raws[1][:, 0, :]))
+        nc.vector.tensor_copy(out=by_column(g_t1[:, 1]), in_=by_row(tail_raws[1][:, 1, :]))
+        codes, scales = quantise(previous, BLOCK, codep)
+        multiply(UNITS - TAIL_UNITS - BLOCK, BLOCK, codes, scales, NBLOCK)
+        relu_and_store(NBLOCK + RELU_LAG)
+        codes, scales = quantise(g_t0, 2, code2p)
+        multiply(UNITS - 4, 2, codes, scales, NBLOCK)
+        codes, scales = quantise(g_t1, 2, code2p)
+        multiply(UNITS - 2, 2, codes, scales, NBLOCK)
+        relu_and_store(NBLOCK + RELU_LAG)

@@ -44,7 +44,6 @@ def by_row(raw):
 def tile_blockrf_kernel(tc, x, gamma, beta, moving_mean, moving_var, weight, out):
     nc = tc.nc
     with ExitStack() as ctx:
-        ctx.enter_context(tc.manual_schedule())
         const = ctx.enter_context(tc.tile_pool(name="const", bufs=1))
         xwork = ctx.enter_context(tc.tile_pool(name="xwork", bufs=3))
         rawp = ctx.enter_context(tc.tile_pool(name="rawp", bufs=RAW_BUFS))

@@ -34,11 +34,11 @@ RELU_LAG = 2
 
 
 def by_column(grouped):
-    return grouped.rearrange("p (c i) t -> p c t i", i=4)
+    return grouped.rearrange("p (c i) t -> p c t i", i=8)
 
 
 def by_row(raw):
-    return raw.rearrange("p (t c i) -> p c t i", t=PACK, i=4)
+    return raw.rearrange("p (t c i) -> p c t i", t=PACK, i=8)
 
 
 def tile_blockrf_kernel(tc, x, gamma, beta, moving_mean, moving_var, weight, out):
@@ -179,7 +179,7 @@ def tile_blockrf_kernel(tc, x, gamma, beta, moving_mean, moving_var, weight, out
         def x_regroup(g):
             gx = xwork.tile([P, XG * B, PACK], BF16, name="gx", align_bytes=64)
             gxs[g] = gx
-            nc.vector.tensor_copy(out=by_column(gx[:]), in_=xn[g][:].rearrange("p t (c i) -> p c t i", i=4))
+            nc.vector.tensor_copy(out=by_column(gx[:]), in_=xn[g][:].rearrange("p t (c i) -> p c t i", i=8))
 
         def x_quantise(g):
             cols = slice(g * XG * B, (g + 1) * XG * B)
@@ -197,8 +197,8 @@ def tile_blockrf_kernel(tc, x, gamma, beta, moving_mean, moving_var, weight, out
         x_regroup(1)
         x_quantise(0)
         g_h1 = grp2.tile([P, 2, F, PACK], BF16, name="g2", align_bytes=64)
-        nc.vector.tensor_copy(out=g_h1[:].rearrange("p u (c i) t -> p u c t i", i=4),
-                              in_=raw_h1[:].rearrange("p u (t c i) -> p u c t i", t=PACK, i=4))
+        nc.vector.tensor_copy(out=g_h1[:].rearrange("p u (c i) t -> p u c t i", i=8),
+                              in_=raw_h1[:].rearrange("p u (t c i) -> p u c t i", t=PACK, i=8))
         batch_norm(2)
         transposes(4)
         x_regroup(2)
@@ -222,8 +222,8 @@ def tile_blockrf_kernel(tc, x, gamma, beta, moving_mean, moving_var, weight, out
             g4 = grp.tile([P, BLOCK, F, PACK], BF16, name="g4", align_bytes=64)
             for k in range(2):
                 nc.scalar.copy(out=by_column(g4[:, k]), in_=by_row(raw[:, k, :]))
-            nc.vector.tensor_copy(out=g4[:, 2:4].rearrange("p u (c i) t -> p u c t i", i=4),
-                                  in_=raw[:, 2:4, :].rearrange("p u (t c i) -> p u c t i", t=PACK, i=4))
+            nc.vector.tensor_copy(out=g4[:, 2:4].rearrange("p u (c i) t -> p u c t i", i=8),
+                                  in_=raw[:, 2:4, :].rearrange("p u (t c i) -> p u c t i", t=PACK, i=8))
             if b + RAW_BUFS < NBLOCK:
                 raws.append(load_block(b + RAW_BUFS))
             elif len(tail_raws) == 0:

@@ -31,6 +31,8 @@ NBLOCK = (UNITS - HEAD_UNITS - TAIL_UNITS) // BLOCK
 RAW_BUFS = 7
 V_BANKS = ((0, 1), (1, 1))
 RELU_LAG = 2
+HALF = F // 2
+S3_BLOCKS = (7,)
 
 
 def by_column(grouped):
@@ -53,6 +55,7 @@ def tile_blockrf_kernel(tc, x, gamma, beta, moving_mean, moving_var, weight, out
         codep = ctx.enter_context(tc.tile_pool(name="codep", bufs=4))
         code2p = ctx.enter_context(tc.tile_pool(name="code2p", bufs=2))
         outp = ctx.enter_context(tc.tile_pool(name="outp", bufs=4))
+        tailp = ctx.enter_context(tc.tile_pool(name="tailp", bufs=1))
         xps = ctx.enter_context(tc.psum_pool(name="xps", bufs=4))
         accp = ctx.enter_context(tc.psum_pool(name="accp", bufs=4))
 
@@ -98,6 +101,7 @@ def tile_blockrf_kernel(tc, x, gamma, beta, moving_mean, moving_var, weight, out
         x_codes = const.tile([P, NPOS * B], U32, name="x_codes", align_bytes=64)
         x_scales = const.tile([P, NPOS * B], U8, name="x_scales", align_bytes=64)
         accs = {}
+        last_accs = []
         finished = []
         stored = {"n": 0}
 
@@ -108,21 +112,34 @@ def tile_blockrf_kernel(tc, x, gamma, beta, moving_mean, moving_var, weight, out
                                   in_=grouped[:].rearrange("p u c t -> p (u c t)"))
             return codes, scales
 
+        def one_pass(unit, acc_ap, codes, scales, cols, start, stop):
+            o, tap = divmod(unit, TAPS)
+            pos = (o // OW + tap // KW) * W + (o % OW + tap % KW)
+            nc.tensor.matmul_mx(out=acc_ap,
+                                lhsT=x_codes[:, pos * B:(pos + 1) * B].bitcast(FP8X4),
+                                lhsT_scale=x_scales[:, pos * B:(pos + 1) * B],
+                                rhs=codes[:, cols].bitcast(FP8X4), rhs_scale=scales[:, cols],
+                                start=start, stop=stop)
+
         def multiply(first, units, codes, scales, step):
             for k in range(units):
                 o, tap = divmod(first + k, TAPS)
-                pos = (o // OW + tap // KW) * W + (o % OW + tap % KW)
-                if tap == 0:
-                    acc = accp.tile([P, F], F32, name="acc")
-                    accs[o] = acc
-                nc.tensor.matmul_mx(out=accs[o][:],
-                                    lhsT=x_codes[:, pos * B:(pos + 1) * B].bitcast(FP8X4),
-                                    lhsT_scale=x_scales[:, pos * B:(pos + 1) * B],
-                                    rhs=codes[:, k * F:(k + 1) * F].bitcast(FP8X4),
-                                    rhs_scale=scales[:, k * F:(k + 1) * F],
-                                    start=(tap == 0), stop=(tap == TAPS - 1))
-                if tap == TAPS - 1:
-                    finished.append((o, step))
+                if o == NOUT - 1:
+                    if tap == 0:
+                        for h in range(2):
+                            acc_h = accp.tile([P, HALF], F32, name="acc")
+                            last_accs.append(acc_h)
+                    for h in range(2):
+                        one_pass(first + k, last_accs[h][:], codes, scales,
+                                 slice(k * F + h * HALF, k * F + (h + 1) * HALF), tap == 0, False)
+                else:
+                    if tap == 0:
+                        acc = accp.tile([P, F], F32, name="acc")
+                        accs[o] = acc
+                    one_pass(first + k, accs[o][:], codes, scales, slice(k * F, (k + 1) * F),
+                             tap == 0, tap == TAPS - 1)
+                    if tap == TAPS - 1:
+                        finished.append((o, step))
 
         def relu_and_store(step):
             for idx in range(stored["n"], len(finished)):
@@ -220,10 +237,14 @@ def tile_blockrf_kernel(tc, x, gamma, beta, moving_mean, moving_var, weight, out
         for b in range(NBLOCK):
             raw = raws[b]
             g4 = grp.tile([P, BLOCK, F, PACK], BF16, name="g4", align_bytes=64)
-            for k in range(2):
-                nc.scalar.copy(out=by_column(g4[:, k]), in_=by_row(raw[:, k, :]))
-            nc.vector.tensor_copy(out=g4[:, 2:4].rearrange("p u (c i) t -> p u c t i", i=8),
-                                  in_=raw[:, 2:4, :].rearrange("p u (t c i) -> p u c t i", t=PACK, i=8))
+            nc.scalar.copy(out=g4[:, 0:2].rearrange("p u (c i) t -> p u c t i", i=8),
+                           in_=raw[:, 0:2, :].rearrange("p u (t c i) -> p u c t i", t=PACK, i=8))
+            if b in S3_BLOCKS:
+                nc.scalar.copy(out=by_column(g4[:, 2]), in_=by_row(raw[:, 2, :]))
+                nc.vector.tensor_copy(out=by_column(g4[:, 3]), in_=by_row(raw[:, 3, :]))
+            else:
+                nc.vector.tensor_copy(out=g4[:, 2:4].rearrange("p u (c i) t -> p u c t i", i=8),
+                                      in_=raw[:, 2:4, :].rearrange("p u (t c i) -> p u c t i", t=PACK, i=8))
             if b + RAW_BUFS < NBLOCK:
                 raws.append(load_block(b + RAW_BUFS))
             elif len(tail_raws) == 0:
@@ -242,15 +263,30 @@ def tile_blockrf_kernel(tc, x, gamma, beta, moving_mean, moving_var, weight, out
 
         g_t0 = grp2.tile([P, 2, F, PACK], BF16, name="g2", align_bytes=64)
         g_t1 = grp2.tile([P, 2, F, PACK], BF16, name="g2", align_bytes=64)
-        for k in range(2):
-            nc.scalar.copy(out=by_column(g_t0[:, k]), in_=by_row(tail_raws[0][:, k, :]))
-        nc.scalar.copy(out=by_column(g_t1[:, 0]), in_=by_row(tail_raws[1][:, 0, :]))
-        nc.vector.tensor_copy(out=by_column(g_t1[:, 1]), in_=by_row(tail_raws[1][:, 1, :]))
+        nc.vector.tensor_copy(out=g_t1[:].rearrange("p u (c i) t -> p u c t i", i=8),
+                              in_=tail_raws[1][:].rearrange("p u (t c i) -> p u c t i", t=PACK, i=8))
+        nc.scalar.copy(out=by_column(g_t0[:, 0]), in_=by_row(tail_raws[0][:, 0, :]))
+        runs = HALF // 8
+        for h in range(2):
+            nc.scalar.copy(out=by_column(g_t0[:, 1])[:, h * runs:(h + 1) * runs],
+                           in_=by_row(tail_raws[0][:, 1, :])[:, h * runs:(h + 1) * runs])
         codes, scales = quantise(previous, BLOCK, codep)
         multiply(UNITS - TAIL_UNITS - BLOCK, BLOCK, codes, scales, NBLOCK)
         relu_and_store(NBLOCK + RELU_LAG)
-        codes, scales = quantise(g_t0, 2, code2p)
-        multiply(UNITS - 4, 2, codes, scales, NBLOCK)
         codes, scales = quantise(g_t1, 2, code2p)
         multiply(UNITS - 2, 2, codes, scales, NBLOCK)
-        relu_and_store(NBLOCK + RELU_LAG)
+        codes1 = tailp.tile([P, F], U32, name="codes1", align_bytes=64)
+        scales1 = tailp.tile([P, F], U8, name="scales1", align_bytes=64)
+        nc.vector.quantize_mx(out=codes1[:].bitcast(FP8X4), scales=scales1[:],
+                              in_=g_t0[:, 0].rearrange("p c t -> p (c t)"))
+        multiply(UNITS - 4, 1, codes1, scales1, NBLOCK)
+        for h in range(2):
+            codes_h = tailp.tile([P, HALF], U32, name="codes_h%d" % h, align_bytes=64)
+            scales_h = tailp.tile([P, HALF], U8, name="scales_h%d" % h, align_bytes=64)
+            nc.vector.quantize_mx(out=codes_h[:].bitcast(FP8X4), scales=scales_h[:],
+                                  in_=g_t0[:, 1, h * HALF:(h + 1) * HALF, :].rearrange("p c t -> p (c t)"))
+            one_pass(UNITS - 3, last_accs[h][:], codes_h, scales_h, slice(0, HALF), False, True)
+        for h in range(2):
+            o_h = outp.tile([P, HALF], F32, name="o_sb")
+            nc.scalar.activation(out=o_h[:], in_=last_accs[h][:], func=ACT.Relu)
+            nc.sync.dma_start(out=out_view[:, NOUT - 1, h * HALF:(h + 1) * HALF], in_=o_h[:])

@@ -32,7 +32,8 @@ RAW_BUFS = 7
 V_BANKS = ((0, 1), (1, 1))
 RELU_LAG = 2
 HALF = F // 2
-S3_BLOCKS = (7,)
+S3_BLOCKS = (4,)
+HALF_BLOCKS = (11,)
 
 
 def by_column(grouped):
@@ -241,6 +242,12 @@ def tile_blockrf_kernel(tc, x, gamma, beta, moving_mean, moving_var, weight, out
                            in_=raw[:, 0:2, :].rearrange("p u (t c i) -> p u c t i", t=PACK, i=8))
             if b in S3_BLOCKS:
                 nc.scalar.copy(out=by_column(g4[:, 2]), in_=by_row(raw[:, 2, :]))
+                nc.vector.tensor_copy(out=by_column(g4[:, 3]), in_=by_row(raw[:, 3, :]))
+            elif b in HALF_BLOCKS:
+                half_runs = HALF // 8
+                nc.scalar.copy(out=by_column(g4[:, 2])[:, 0:half_runs], in_=by_row(raw[:, 2, :])[:, 0:half_runs])
+                nc.vector.tensor_copy(out=by_column(g4[:, 2])[:, half_runs:2 * half_runs],
+                                      in_=by_row(raw[:, 2, :])[:, half_runs:2 * half_runs])
                 nc.vector.tensor_copy(out=by_column(g4[:, 3]), in_=by_row(raw[:, 3, :]))
             else:
                 nc.vector.tensor_copy(out=g4[:, 2:4].rearrange("p u (c i) t -> p u c t i", i=8),

@@ -32,8 +32,10 @@ RAW_BUFS = 7
 V_BANKS = ((0, 1), (1, 1))
 RELU_LAG = 2
 HALF = F // 2
-S3_BLOCKS = (4,)
-HALF_BLOCKS = (11,)
+RUN = 8
+S_COLS = 136
+S_COLS_LOW = 128
+LOW_EVERY = 4
 
 
 def by_column(grouped):
@@ -238,20 +240,11 @@ def tile_blockrf_kernel(tc, x, gamma, beta, moving_mean, moving_var, weight, out
         for b in range(NBLOCK):
             raw = raws[b]
             g4 = grp.tile([P, BLOCK, F, PACK], BF16, name="g4", align_bytes=64)
-            nc.scalar.copy(out=g4[:, 0:2].rearrange("p u (c i) t -> p u c t i", i=8),
-                           in_=raw[:, 0:2, :].rearrange("p u (t c i) -> p u c t i", t=PACK, i=8))
-            if b in S3_BLOCKS:
-                nc.scalar.copy(out=by_column(g4[:, 2]), in_=by_row(raw[:, 2, :]))
-                nc.vector.tensor_copy(out=by_column(g4[:, 3]), in_=by_row(raw[:, 3, :]))
-            elif b in HALF_BLOCKS:
-                half_runs = HALF // 8
-                nc.scalar.copy(out=by_column(g4[:, 2])[:, 0:half_runs], in_=by_row(raw[:, 2, :])[:, 0:half_runs])
-                nc.vector.tensor_copy(out=by_column(g4[:, 2])[:, half_runs:2 * half_runs],
-                                      in_=by_row(raw[:, 2, :])[:, half_runs:2 * half_runs])
-                nc.vector.tensor_copy(out=by_column(g4[:, 3]), in_=by_row(raw[:, 3, :]))
-            else:
-                nc.vector.tensor_copy(out=g4[:, 2:4].rearrange("p u (c i) t -> p u c t i", i=8),
-                                      in_=raw[:, 2:4, :].rearrange("p u (t c i) -> p u c t i", t=PACK, i=8))
+            runs = (S_COLS_LOW if b % LOW_EVERY == 0 else S_COLS) // RUN
+            dst = g4[:].rearrange("p u (c i) t -> p u c t i", i=RUN)
+            src = raw[:].rearrange("p u (t c i) -> p u c t i", t=PACK, i=RUN)
+            nc.scalar.copy(out=dst[:, :, 0:runs], in_=src[:, :, 0:runs])
+            nc.vector.tensor_copy(out=dst[:, :, runs:F // RUN], in_=src[:, :, runs:F // RUN])
             if b + RAW_BUFS < NBLOCK:
                 raws.append(load_block(b + RAW_BUFS))
             elif len(tail_raws) == 0:

@@ -36,6 +36,9 @@ RUN = 8
 S_COLS = 136
 S_COLS_LOW = 128
 LOW_EVERY = 4
+PE_BLOCKS = (1, 3, 5, 7, 9, 11, 13)
+PE_LEAD = 2
+PE_S_COLS = (112, 128)
 
 
 def by_column(grouped):
@@ -100,6 +103,8 @@ def tile_blockrf_kernel(tc, x, gamma, beta, moving_mean, moving_var, weight, out
         nc.scalar.activation(out=warm2[:], in_=warm[:], func=ACT.Sqrt)
         ident = const.tile([P, P], F32, name="ident")
         make_identity(nc, ident[:])
+        ident_bf = const.tile([P, P], BF16, name="ident_bf")
+        nc.vector.tensor_copy(out=ident_bf[:], in_=ident[:])
 
         x_codes = const.tile([P, NPOS * B], U32, name="x_codes", align_bytes=64)
         x_scales = const.tile([P, NPOS * B], U8, name="x_scales", align_bytes=64)
@@ -235,16 +240,39 @@ def tile_blockrf_kernel(tc, x, gamma, beta, moving_mean, moving_var, weight, out
         x_regroup(5)
         x_quantise(4)
 
+        pe_banks = {}
+
+        def tensor_interleave(b):
+            if b in PE_BLOCKS:
+                bank = xps.tile([P, F * PACK], BF16, name="xt")
+                pe_banks[b] = bank
+                src = raws[b][:, 0, :].rearrange("p (t f) -> p t f", t=PACK)
+                dst = bank[:].rearrange("p (f t) -> p t f", t=PACK)
+                for h in range(2):
+                    cols = slice(h * HALF, (h + 1) * HALF)
+                    nc.tensor.matmul(dst[:, :, cols], ident_bf[:], src[:, :, cols], start=True, stop=True)
+
+        for b in range(PE_LEAD):
+            tensor_interleave(b)
         tail_raws = []
         previous = None
         for b in range(NBLOCK):
             raw = raws[b]
             g4 = grp.tile([P, BLOCK, F, PACK], BF16, name="g4", align_bytes=64)
-            runs = (S_COLS_LOW if b % LOW_EVERY == 0 else S_COLS) // RUN
-            dst = g4[:].rearrange("p u (c i) t -> p u c t i", i=RUN)
-            src = raw[:].rearrange("p u (t c i) -> p u c t i", t=PACK, i=RUN)
-            nc.scalar.copy(out=dst[:, :, 0:runs], in_=src[:, :, 0:runs])
-            nc.vector.tensor_copy(out=dst[:, :, runs:F // RUN], in_=src[:, :, runs:F // RUN])
+            if b in PE_BLOCKS:
+                runs = PE_S_COLS[PE_BLOCKS.index(b) % 2] // RUN
+                dst = g4[:, 1:BLOCK].rearrange("p u (c i) t -> p c u t i", i=RUN)
+                src = raw[:, 1:BLOCK, :].rearrange("p u (t c i) -> p c u t i", t=PACK, i=RUN)
+                nc.scalar.copy(out=g4[:, 0].rearrange("p c t -> p (c t)"), in_=pe_banks[b][:])
+                nc.scalar.copy(out=dst[:, 0:runs], in_=src[:, 0:runs])
+                nc.vector.tensor_copy(out=dst[:, runs:F // RUN], in_=src[:, runs:F // RUN])
+            else:
+                runs = (S_COLS_LOW if b % LOW_EVERY == 0 else S_COLS) // RUN
+                dst = g4[:].rearrange("p u (c i) t -> p u c t i", i=RUN)
+                src = raw[:].rearrange("p u (t c i) -> p u c t i", t=PACK, i=RUN)
+                nc.scalar.copy(out=dst[:, :, 0:runs], in_=src[:, :, 0:runs])
+                nc.vector.tensor_copy(out=dst[:, :, runs:F // RUN], in_=src[:, :, runs:F // RUN])
+            tensor_interleave(b + PE_LEAD)
             if b + RAW_BUFS < NBLOCK:
                 raws.append(load_block(b + RAW_BUFS))
             elif len(tail_raws) == 0:

@@ -61,9 +61,10 @@ def tile_blockrf_kernel(tc, x, gamma, beta, moving_mean, moving_var, weight, out
         codep = ctx.enter_context(tc.tile_pool(name="codep", bufs=4))
         code2p = ctx.enter_context(tc.tile_pool(name="code2p", bufs=2))
         outp = ctx.enter_context(tc.tile_pool(name="outp", bufs=4))
-        tailp = ctx.enter_context(tc.tile_pool(name="tailp", bufs=1))
+        tailp = ctx.enter_context(tc.tile_pool(name="tailp", bufs=2))
         xps = ctx.enter_context(tc.psum_pool(name="xps", bufs=4))
-        accp = ctx.enter_context(tc.psum_pool(name="accp", bufs=4))
+        accp = ctx.enter_context(tc.psum_pool(name="accp", bufs=3))
+        pep = ctx.enter_context(tc.psum_pool(name="pep", bufs=1))
 
         w_view = weight.rearrange("o k f -> (o k) f").rearrange("(n p j) f -> p n (j f)", p=P, j=PACK)
         out_view = out.rearrange("b h w f -> b (h w) f")
@@ -109,7 +110,7 @@ def tile_blockrf_kernel(tc, x, gamma, beta, moving_mean, moving_var, weight, out
         x_codes = const.tile([P, NPOS * B], U32, name="x_codes", align_bytes=64)
         x_scales = const.tile([P, NPOS * B], U8, name="x_scales", align_bytes=64)
         accs = {}
-        last_accs = []
+        last_unit = [(o + 1) * TAPS - 1 for o in range(NOUT - 1)] + [UNITS - 3]
         finished = []
         stored = {"n": 0}
 
@@ -132,22 +133,13 @@ def tile_blockrf_kernel(tc, x, gamma, beta, moving_mean, moving_var, weight, out
         def multiply(first, units, codes, scales, step):
             for k in range(units):
                 o, tap = divmod(first + k, TAPS)
-                if o == NOUT - 1:
-                    if tap == 0:
-                        for h in range(2):
-                            acc_h = accp.tile([P, HALF], F32, name="acc")
-                            last_accs.append(acc_h)
-                    for h in range(2):
-                        one_pass(first + k, last_accs[h][:], codes, scales,
-                                 slice(k * F + h * HALF, k * F + (h + 1) * HALF), tap == 0, False)
-                else:
-                    if tap == 0:
-                        acc = accp.tile([P, F], F32, name="acc")
-                        accs[o] = acc
-                    one_pass(first + k, accs[o][:], codes, scales, slice(k * F, (k + 1) * F),
-                             tap == 0, tap == TAPS - 1)
-                    if tap == TAPS - 1:
-                        finished.append((o, step))
+                if tap == 0:
+                    acc = accp.tile([P, F], F32, name="acc")
+                    accs[o] = acc
+                one_pass(first + k, accs[o][:], codes, scales, slice(k * F, (k + 1) * F),
+                         tap == 0, first + k == last_unit[o])
+                if first + k == last_unit[o]:
+                    finished.append((o, step))
 
         def relu_and_store(step):
             for idx in range(stored["n"], len(finished)):
@@ -244,7 +236,7 @@ def tile_blockrf_kernel(tc, x, gamma, beta, moving_mean, moving_var, weight, out
 
         def tensor_interleave(b):
             if b in PE_BLOCKS:
-                bank = xps.tile([P, F * PACK], BF16, name="xt")
+                bank = pep.tile([P, F * PACK], BF16, name="bank")
                 pe_banks[b] = bank
                 src = raws[b][:, 0, :].rearrange("p (t f) -> p t f", t=PACK)
                 dst = bank[:].rearrange("p (f t) -> p t f", t=PACK)
@@ -263,8 +255,8 @@ def tile_blockrf_kernel(tc, x, gamma, beta, moving_mean, moving_var, weight, out
                 runs = PE_S_COLS[PE_BLOCKS.index(b) % 2] // RUN
                 dst = g4[:, 1:BLOCK].rearrange("p u (c i) t -> p c u t i", i=RUN)
                 src = raw[:, 1:BLOCK, :].rearrange("p u (t c i) -> p c u t i", t=PACK, i=RUN)
-                nc.scalar.copy(out=g4[:, 0].rearrange("p c t -> p (c t)"), in_=pe_banks[b][:])
                 nc.scalar.copy(out=dst[:, 0:runs], in_=src[:, 0:runs])
+                nc.scalar.copy(out=g4[:, 0].rearrange("p c t -> p (c t)"), in_=pe_banks[b][:])
                 nc.vector.tensor_copy(out=dst[:, runs:F // RUN], in_=src[:, runs:F // RUN])
             else:
                 runs = (S_COLS_LOW if b % LOW_EVERY == 0 else S_COLS) // RUN
@@ -294,27 +286,16 @@ def tile_blockrf_kernel(tc, x, gamma, beta, moving_mean, moving_var, weight, out
         nc.vector.tensor_copy(out=g_t1[:].rearrange("p u (c i) t -> p u c t i", i=8),
                               in_=tail_raws[1][:].rearrange("p u (t c i) -> p u c t i", t=PACK, i=8))
         nc.scalar.copy(out=by_column(g_t0[:, 0]), in_=by_row(tail_raws[0][:, 0, :]))
-        runs = HALF // 8
-        for h in range(2):
-            nc.scalar.copy(out=by_column(g_t0[:, 1])[:, h * runs:(h + 1) * runs],
-                           in_=by_row(tail_raws[0][:, 1, :])[:, h * runs:(h + 1) * runs])
+        nc.scalar.copy(out=by_column(g_t0[:, 1]), in_=by_row(tail_raws[0][:, 1, :]))
         codes, scales = quantise(previous, BLOCK, codep)
         multiply(UNITS - TAIL_UNITS - BLOCK, BLOCK, codes, scales, NBLOCK)
         relu_and_store(NBLOCK + RELU_LAG)
         codes, scales = quantise(g_t1, 2, code2p)
         multiply(UNITS - 2, 2, codes, scales, NBLOCK)
-        codes1 = tailp.tile([P, F], U32, name="codes1", align_bytes=64)
-        scales1 = tailp.tile([P, F], U8, name="scales1", align_bytes=64)
-        nc.vector.quantize_mx(out=codes1[:].bitcast(FP8X4), scales=scales1[:],
-                              in_=g_t0[:, 0].rearrange("p c t -> p (c t)"))
-        multiply(UNITS - 4, 1, codes1, scales1, NBLOCK)
-        for h in range(2):
-            codes_h = tailp.tile([P, HALF], U32, name="codes_h%d" % h, align_bytes=64)
-            scales_h = tailp.tile([P, HALF], U8, name="scales_h%d" % h, align_bytes=64)
-            nc.vector.quantize_mx(out=codes_h[:].bitcast(FP8X4), scales=scales_h[:],
-                                  in_=g_t0[:, 1, h * HALF:(h + 1) * HALF, :].rearrange("p c t -> p (c t)"))
-            one_pass(UNITS - 3, last_accs[h][:], codes_h, scales_h, slice(0, HALF), False, True)
-        for h in range(2):
-            o_h = outp.tile([P, HALF], F32, name="o_sb")
-            nc.scalar.activation(out=o_h[:], in_=last_accs[h][:], func=ACT.Relu)
-            nc.sync.dma_start(out=out_view[:, NOUT - 1, h * HALF:(h + 1) * HALF], in_=o_h[:])
+        for k in range(2):
+            codes1 = tailp.tile([P, F], U32, name="codes1", align_bytes=64)
+            scales1 = tailp.tile([P, F], U8, name="scales1", align_bytes=64)
+            nc.vector.quantize_mx(out=codes1[:].bitcast(FP8X4), scales=scales1[:],
+                                  in_=g_t0[:, k].rearrange("p c t -> p (c t)"))
+            multiply(UNITS - 4 + k, 1, codes1, scales1, NBLOCK)
+        relu_and_store(NBLOCK + RELU_LAG)

@@ -33,12 +33,10 @@ V_BANKS = ((0, 1), (1, 1))
 RELU_LAG = 2
 HALF = F // 2
 RUN = 8
-S_COLS = 136
-S_COLS_LOW = 128
-LOW_EVERY = 4
+S_COLS = 128
 PE_BLOCKS = (1, 3, 5, 7, 9, 11, 13)
 PE_LEAD = 2
-PE_S_COLS = (112, 128)
+PE_S_COLS = 112
 
 
 def by_column(grouped):
@@ -252,14 +250,14 @@ def tile_blockrf_kernel(tc, x, gamma, beta, moving_mean, moving_var, weight, out
             raw = raws[b]
             g4 = grp.tile([P, BLOCK, F, PACK], BF16, name="g4", align_bytes=64)
             if b in PE_BLOCKS:
-                runs = PE_S_COLS[PE_BLOCKS.index(b) % 2] // RUN
+                runs = PE_S_COLS // RUN
                 dst = g4[:, 1:BLOCK].rearrange("p u (c i) t -> p c u t i", i=RUN)
                 src = raw[:, 1:BLOCK, :].rearrange("p u (t c i) -> p c u t i", t=PACK, i=RUN)
                 nc.scalar.copy(out=dst[:, 0:runs], in_=src[:, 0:runs])
                 nc.scalar.copy(out=g4[:, 0].rearrange("p c t -> p (c t)"), in_=pe_banks[b][:])
                 nc.vector.tensor_copy(out=dst[:, runs:F // RUN], in_=src[:, runs:F // RUN])
             else:
-                runs = (S_COLS_LOW if b % LOW_EVERY == 0 else S_COLS) // RUN
+                runs = S_COLS // RUN
                 dst = g4[:].rearrange("p u (c i) t -> p u c t i", i=RUN)
                 src = raw[:].rearrange("p u (t c i) -> p u c t i", t=PACK, i=RUN)
                 nc.scalar.copy(out=dst[:, :, 0:runs], in_=src[:, :, 0:runs])

from contextlib import ExitStack

import concourse.mybir as mybir
from concourse.masks import make_identity

F32 = mybir.dt.float32
BF16 = mybir.dt.bfloat16
U32 = mybir.dt.uint32
U8 = mybir.dt.uint8
FP8X4 = mybir.dt.float8_e4m3fn_x4
ACT = mybir.ActivationFunctionType
ALU = mybir.AluOpType

P = 128
PACK = 4
B, H, W, C, F, KH, KW = 128, 4, 6, 512, 256, 3, 3
OH, OW = H - KH + 1, W - KW + 1
NPOS = H * W
TAPS = KH * KW
NOUT = OH * OW
UNITS = NOUT * TAPS
BN_EPS = 1e-3
FLOPS = 2 * B * NOUT * TAPS * C * F

XG = 4
NG = NPOS // XG
HEAD_UNITS = 4
TAIL_UNITS = 4
BLOCK = 4
NBLOCK = (UNITS - HEAD_UNITS - TAIL_UNITS) // BLOCK
RAW_BUFS = 7
V_BANKS = ((0, 1), (1, 1))
RELU_LAG = 2
HALF = F // 2
RUN = 8
S_COLS = 128
PE_BLOCKS = (1, 3, 5, 7, 9, 11, 13)
PE_LEAD = 2
PE_S_COLS = 112


def by_column(grouped):
    return grouped.rearrange("p (c i) t -> p c t i", i=8)


def by_row(raw):
    return raw.rearrange("p (t c i) -> p c t i", t=PACK, i=8)


def tile_blockrf_kernel(tc, x, gamma, beta, moving_mean, moving_var, weight, out):
    nc = tc.nc
    with ExitStack() as ctx:
        const = ctx.enter_context(tc.tile_pool(name="const", bufs=1))
        xwork = ctx.enter_context(tc.tile_pool(name="xwork", bufs=3))
        rawp = ctx.enter_context(tc.tile_pool(name="rawp", bufs=RAW_BUFS))
        raw2p = ctx.enter_context(tc.tile_pool(name="raw2p", bufs=2))
        grp = ctx.enter_context(tc.tile_pool(name="grp", bufs=4))
        grp2 = ctx.enter_context(tc.tile_pool(name="grp2", bufs=2))
        codep = ctx.enter_context(tc.tile_pool(name="codep", bufs=4))
        code2p = ctx.enter_context(tc.tile_pool(name="code2p", bufs=2))
        outp = ctx.enter_context(tc.tile_pool(name="outp", bufs=4))
        tailp = ctx.enter_context(tc.tile_pool(name="tailp", bufs=2))
        xps = ctx.enter_context(tc.psum_pool(name="xps", bufs=4))
        accp = ctx.enter_context(tc.psum_pool(name="accp", bufs=3))
        pep = ctx.enter_context(tc.psum_pool(name="pep", bufs=1))

        w_view = weight.rearrange("o k f -> (o k) f").rearrange("(n p j) f -> p n (j f)", p=P, j=PACK)
        out_view = out.rearrange("b h w f -> b (h w) f")
        x_flat = x.rearrange("b h w c -> b (h w c)")

        def load_pair(first, dmas):
            raw = raw2p.tile([P, 2, PACK * F], BF16, name="raw2")
            step = 2 // dmas
            for d in range(dmas):
                nc.sync.dma_start(out=raw[:, d * step:(d + 1) * step, :],
                                  in_=w_view[:, first + d * step:first + (d + 1) * step, :])
            return raw

        def load_block(b):
            raw = rawp.tile([P, BLOCK, PACK * F], BF16, name="raw")
            first = HEAD_UNITS + b * BLOCK
            nc.sync.dma_start(out=raw[:], in_=w_view[:, first:first + BLOCK, :])
            return raw

        g_t = const.tile([P, PACK], BF16, name="g_t")
        b_t = const.tile([P, PACK], BF16, name="b_t")
        m_t = const.tile([P, PACK], BF16, name="m_t")
        v_t = const.tile([P, PACK], BF16, name="v_t")
        for dst, src in ((v_t, moving_var), (g_t, gamma), (m_t, moving_mean), (b_t, beta)):
            nc.scalar.dma_start(out=dst[:], in_=src.rearrange("(p t) -> p t", t=PACK))
        raw_h0 = load_pair(0, 2)
        x_sb = const.tile([P, NPOS * C], BF16, name="x_sb")
        for g in range(NG):
            cols = slice(g * XG * C, (g + 1) * XG * C)
            nc.sync.dma_start(out=x_sb[:, cols], in_=x_flat[:, cols])
        raw_h1 = load_pair(2, 1)
        raws = [load_block(b) for b in range(RAW_BUFS)]

        warm = const.tile([P, 1], F32, name="warm")
        warm2 = const.tile([P, 1], F32, name="warm2")
        nc.vector.memset(warm[:], 1.0)
        nc.scalar.activation(out=warm2[:], in_=warm[:], func=ACT.Sqrt)
        ident = const.tile([P, P], F32, name="ident")
        make_identity(nc, ident[:])
        ident_bf = const.tile([P, P], BF16, name="ident_bf")
        nc.vector.tensor_copy(out=ident_bf[:], in_=ident[:])

        x_codes = const.tile([P, NPOS * B], U32, name="x_codes", align_bytes=64)
        x_scales = const.tile([P, NPOS * B], U8, name="x_scales", align_bytes=64)
        accs = {}
        last_unit = [(o + 1) * TAPS - 1 for o in range(NOUT - 1)] + [UNITS - 3]
        finished = []
        stored = {"n": 0}

        def quantise(grouped, units, pool):
            codes = pool.tile([P, units * F], U32, name="codes%d" % units, align_bytes=64)
            scales = pool.tile([P, units * F], U8, name="scales%d" % units, align_bytes=64)
            nc.vector.quantize_mx(out=codes[:].bitcast(FP8X4), scales=scales[:],
                                  in_=grouped[:].rearrange("p u c t -> p (u c t)"))
            return codes, scales

        def one_pass(unit, acc_ap, codes, scales, cols, start, stop):
            o, tap = divmod(unit, TAPS)
            pos = (o // OW + tap // KW) * W + (o % OW + tap % KW)
            nc.tensor.matmul_mx(out=acc_ap,
                                lhsT=x_codes[:, pos * B:(pos + 1) * B].bitcast(FP8X4),
                                lhsT_scale=x_scales[:, pos * B:(pos + 1) * B],
                                rhs=codes[:, cols].bitcast(FP8X4), rhs_scale=scales[:, cols],
                                start=start, stop=stop)

        def multiply(first, units, codes, scales, step):
            for k in range(units):
                o, tap = divmod(first + k, TAPS)
                if tap == 0:
                    acc = accp.tile([P, F], F32, name="acc")
                    accs[o] = acc
                one_pass(first + k, accs[o][:], codes, scales, slice(k * F, (k + 1) * F),
                         tap == 0, first + k == last_unit[o])
                if first + k == last_unit[o]:
                    finished.append((o, step))

        def relu_and_store(step):
            for idx in range(stored["n"], len(finished)):
                o, when = finished[idx]
                if step - when >= RELU_LAG:
                    o_sb = outp.tile([P, F], F32, name="o_sb")
                    nc.scalar.activation(out=o_sb[:], in_=accs[o][:], func=ACT.Relu)
                    nc.sync.dma_start(out=out_view[:, o, :], in_=o_sb[:])
                    stored["n"] = idx + 1

        veps = const.tile([P, PACK], F32, name="veps")
        sd = const.tile([P, PACK], F32, name="sd")
        rs = const.tile([P, PACK], F32, name="rs")
        inv = const.tile([P, PACK], F32, name="inv")
        mi = const.tile([P, PACK], F32, name="mi")
        shift = const.tile([P, PACK], F32, name="shift")
        nc.vector.tensor_scalar(out=veps[:], in0=v_t[:], scalar1=BN_EPS, scalar2=None, op0=ALU.add)
        nc.scalar.activation(out=sd[:], in_=veps[:], func=ACT.Sqrt)
        g_h0 = grp2.tile([P, 2, F, PACK], BF16, name="g2", align_bytes=64)
        nc.vector.tensor_copy(out=by_column(g_h0[:, 0]), in_=by_row(raw_h0[:, 0, :]))
        nc.scalar.copy(out=by_column(g_h0[:, 1]), in_=by_row(raw_h0[:, 1, :]))
        nc.vector.reciprocal(out=rs[:], in_=sd[:])
        nc.vector.tensor_tensor(out=inv[:], in0=g_t[:], in1=rs[:], op=ALU.mult)
        nc.vector.tensor_tensor(out=mi[:], in0=m_t[:], in1=inv[:], op=ALU.mult)
        nc.vector.tensor_tensor(out=shift[:], in0=b_t[:], in1=mi[:], op=ALU.subtract)

        x_words = x_sb[:].bitcast(F32).rearrange("b (q w u) -> b q u w", w=P, u=2)
        banks = {}
        xn = {}
        gxs = {}

        def transposes(g):
            for u in range(2):
                xt = xps.tile([P, XG * B], F32, name="xt")
                for j in range(XG):
                    nc.tensor.transpose(xt[:, j * B:(j + 1) * B], x_words[:, g * XG + j, u, :], ident[:])
                banks[(g, u)] = xt

        def batch_norm(g):
            xn_t = xwork.tile([P, PACK, XG * B], BF16, name="xn_t")
            xn[g] = xn_t
            for u in range(2):
                halves = banks[(g, u)][:].bitcast(BF16).rearrange("p (n e) -> p n e", e=2)
                for e in range(2):
                    t = 2 * u + e
                    if (g, u) in V_BANKS:
                        nc.vector.tensor_scalar(out=xn_t[:, t, :], in0=halves[:, :, e],
                                                scalar1=inv[:, t:t + 1], scalar2=shift[:, t:t + 1],
                                                op0=ALU.mult, op1=ALU.add)
                    else:
                        nc.scalar.activation(out=xn_t[:, t, :], in_=halves[:, :, e], func=ACT.Identity,
                                             bias=shift[:, t:t + 1], scale=inv[:, t:t + 1])

        def x_regroup(g):
            gx = xwork.tile([P, XG * B, PACK], BF16, name="gx", align_bytes=64)
            gxs[g] = gx
            nc.vector.tensor_copy(out=by_column(gx[:]), in_=xn[g][:].rearrange("p t (c i) -> p c t i", i=8))

        def x_quantise(g):
            cols = slice(g * XG * B, (g + 1) * XG * B)
            nc.vector.quantize_mx(out=x_codes[:, cols].bitcast(FP8X4), scales=x_scales[:, cols],
                                  in_=gxs[g][:].rearrange("p c t -> p (c t)"))

        transposes(0)
        transposes(1)
        q_h0 = quantise(g_h0, 2, code2p)
        batch_norm(0)
        transposes(2)
        x_regroup(0)
        batch_norm(1)
        transposes(3)
        x_regroup(1)
        x_quantise(0)
        g_h1 = grp2.tile([P, 2, F, PACK], BF16, name="g2", align_bytes=64)
        nc.vector.tensor_copy(out=g_h1[:].rearrange("p u (c i) t -> p u c t i", i=8),
                              in_=raw_h1[:].rearrange("p u (t c i) -> p u c t i", t=PACK, i=8))
        batch_norm(2)
        transposes(4)
        x_regroup(2)
        x_quantise(1)
        q_h1 = quantise(g_h1, 2, code2p)
        batch_norm(3)
        transposes(5)
        x_regroup(3)
        x_quantise(2)
        batch_norm(4)
        x_regroup(4)
        x_quantise(3)
        batch_norm(5)
        x_regroup(5)
        x_quantise(4)

        pe_banks = {}

        def tensor_interleave(b):
            if b in PE_BLOCKS:
                bank = pep.tile([P, F * PACK], BF16, name="bank")
                pe_banks[b] = bank
                src = raws[b][:, 0, :].rearrange("p (t f) -> p t f", t=PACK)
                dst = bank[:].rearrange("p (f t) -> p t f", t=PACK)
                for h in range(2):
                    cols = slice(h * HALF, (h + 1) * HALF)
                    nc.tensor.matmul(dst[:, :, cols], ident_bf[:], src[:, :, cols], start=True, stop=True)

        for b in range(PE_LEAD):
            tensor_interleave(b)
        tail_raws = []
        previous = None
        for b in range(NBLOCK):
            raw = raws[b]
            g4 = grp.tile([P, BLOCK, F, PACK], BF16, name="g4", align_bytes=64)
            if b in PE_BLOCKS:
                runs = PE_S_COLS // RUN
                dst = g4[:, 1:BLOCK].rearrange("p u (c i) t -> p c u t i", i=RUN)
                src = raw[:, 1:BLOCK, :].rearrange("p u (t c i) -> p c u t i", t=PACK, i=RUN)
                nc.scalar.copy(out=dst[:, 0:runs], in_=src[:, 0:runs])
                nc.scalar.copy(out=g4[:, 0].rearrange("p c t -> p (c t)"), in_=pe_banks[b][:])
                nc.vector.tensor_copy(out=dst[:, runs:F // RUN], in_=src[:, runs:F // RUN])
            else:
                runs = S_COLS // RUN
                dst = g4[:].rearrange("p u (c i) t -> p u c t i", i=RUN)
                src = raw[:].rearrange("p u (t c i) -> p u c t i", t=PACK, i=RUN)
                nc.scalar.copy(out=dst[:, :, 0:runs], in_=src[:, :, 0:runs])
                nc.vector.tensor_copy(out=dst[:, :, runs:F // RUN], in_=src[:, :, runs:F // RUN])
            tensor_interleave(b + PE_LEAD)
            if b + RAW_BUFS < NBLOCK:
                raws.append(load_block(b + RAW_BUFS))
            elif len(tail_raws) == 0:
                tail_raws.append(load_pair(UNITS - 4, 1))
            elif len(tail_raws) == 1:
                tail_raws.append(load_pair(UNITS - 2, 2))
            if b == 0:
                x_quantise(5)
                multiply(0, 2, q_h0[0], q_h0[1], b)
                multiply(2, 2, q_h1[0], q_h1[1], b)
            relu_and_store(b)
            if previous is not None:
                codes, scales = quantise(previous, BLOCK, codep)
                multiply(HEAD_UNITS + (b - 1) * BLOCK, BLOCK, codes, scales, b)
            previous = g4

        g_t0 = grp2.tile([P, 2, F, PACK], BF16, name="g2", align_bytes=64)
        g_t1 = grp2.tile([P, 2, F, PACK], BF16, name="g2", align_bytes=64)
        nc.vector.tensor_copy(out=g_t1[:].rearrange("p u (c i) t -> p u c t i", i=8),
                              in_=tail_raws[1][:].rearrange("p u (t c i) -> p u c t i", t=PACK, i=8))
        nc.scalar.copy(out=by_column(g_t0[:, 0]), in_=by_row(tail_raws[0][:, 0, :]))
        nc.scalar.copy(out=by_column(g_t0[:, 1]), in_=by_row(tail_raws[0][:, 1, :]))
        codes, scales = quantise(previous, BLOCK, codep)
        multiply(UNITS - TAIL_UNITS - BLOCK, BLOCK, codes, scales, NBLOCK)
        relu_and_store(NBLOCK + RELU_LAG)
        codes, scales = quantise(g_t1, 2, code2p)
        multiply(UNITS - 2, 2, codes, scales, NBLOCK)
        for k in range(2):
            codes1 = tailp.tile([P, F], U32, name="codes1", align_bytes=64)
            scales1 = tailp.tile([P, F], U8, name="scales1", align_bytes=64)
            nc.vector.quantize_mx(out=codes1[:].bitcast(FP8X4), scales=scales1[:],
                                  in_=g_t0[:, k].rearrange("p c t -> p (c t)"))
            multiply(UNITS - 4 + k, 1, codes1, scales1, NBLOCK)
        relu_and_store(NBLOCK + RELU_LAG)
